import numpy as np
import ml_dtypes


def mxq(x, axis, fmt="e4m3"):
    dtype, down = {"e4m3": (ml_dtypes.float8_e4m3fn, 7), "e5m2": (ml_dtypes.float8_e5m2, 14)}[fmt]
    v = np.moveaxis(np.asarray(x, np.float32).astype(ml_dtypes.bfloat16).astype(np.float64), axis, -1)
    blocks = v.reshape(v.shape[:-1] + (-1, 32))
    amax = np.abs(blocks).max(-1, keepdims=True)
    byte = np.maximum(np.where(amax > 0, np.frexp(amax)[1] - 1 + 127, 0) - down, 1)
    scale = np.exp2(byte - 127.0)
    codes = (blocks / scale).astype(np.float32).astype(dtype).astype(np.float64)
    return np.moveaxis((codes * scale).reshape(v.shape), -1, axis)


WIDE = False


def mx_kscale(k):
    if not WIDE:
        return np.ones(k)
    levels = np.array([10, -10, 5, -5, 0])
    a = np.random.permutation(np.resize(levels, k // 512 * 4)).reshape(k // 512, 4)
    idx = np.arange(k)
    return np.exp2(a[idx // 512, idx % 128 // 32])


BF16 = ml_dtypes.bfloat16


def bf(x):
    return np.asarray(x, np.float32).astype(BF16)


def f64(x):
    return np.asarray(x).astype(np.float64)


E2M1 = np.array([0.0, 0.5, 1.0, 1.5, 2.0, 3.0, 4.0, 6.0, -0.0, -0.5, -1.0, -1.5, -2.0, -3.0, -4.0, -6.0])


def pack_weight(w, fmt):
    k, n = w.shape
    w = f64(bf(w)).reshape(k // 32, 32, n)
    amax = np.abs(w).max(1)
    if fmt == "e4m3":
        byte = np.frexp(amax)[1] - 1 + 127 - 7
    else:
        mant, ex = np.frexp(amax / 6.0)
        byte = np.where(mant > 0.5, ex, ex - 1) + 127
    byte = np.clip(np.where(amax > 0, byte, 1), 1, 254)
    scaled = (w * np.exp2(127.0 - byte)[:, None, :]).reshape(k, n).astype(np.float32)
    by_word = np.ascontiguousarray(scaled.reshape(k // 512, 128, 4, n).transpose(0, 1, 3, 2))
    if fmt == "e4m3":
        words = by_word.astype(ml_dtypes.float8_e4m3fn).view(np.uint8)
    else:
        c = by_word.astype(ml_dtypes.float4_e2m1fn).view(np.uint8) & 0xF
        words = c[..., 0::2] | (c[..., 1::2] << 4)
    return np.ascontiguousarray(words), np.ascontiguousarray(byte.astype(np.uint8).reshape(k // 512, 16, n))


def unpack_weight(words, scales, fmt):
    g, p, n, _ = words.shape
    if fmt == "e4m3":
        vals = np.ascontiguousarray(words).view(ml_dtypes.float8_e4m3fn).astype(np.float64)
    else:
        nib = np.empty((g, p, n, 4), np.uint8)
        nib[..., 0::2] = words & 0xF
        nib[..., 1::2] = words >> 4
        vals = E2M1[nib]
    vals = vals * np.repeat(np.exp2(scales.astype(np.float64) - 127.0), 8, axis=1)[..., None]
    return vals.transpose(0, 1, 3, 2).reshape(g * 512, n)


B, T, D, H, DH, F = 4, 1024, 1024, 4, 64, 4096
A = H * DH
EPS = 1e-6
FMT = "e4m3"


def layer_norm(v, gain, bias):
    mu = v.mean(-1, keepdims=True)
    var = np.square(v - mu).mean(-1, keepdims=True)
    return (v - mu) * (1.0 / np.sqrt(var + EPS)) * gain + bias


def setup_inputs():
    s = mx_kscale(D)
    r = np.random.standard_normal
    x = bf(r((B, T, D)))
    ln1_gain = bf((1.0 + 0.1 * r(D)) * s)
    ln1_bias = bf(0.1 * r(D) * s)
    wq_words, wq_scales = pack_weight(r((D, A)) / np.sqrt(D) / s[:, None], FMT)
    bq = bf(0.1 * r(A))
    wk_words, wk_scales = pack_weight(r((D, A)) / np.sqrt(D) / s[:, None], FMT)
    bk = bf(0.1 * r(A))
    wv_words, wv_scales = pack_weight(r((D, A)) / np.sqrt(D) / s[:, None], FMT)
    bv = bf(0.1 * r(A))
    return {"x": x,
            "ln1_gain": ln1_gain,
            "ln1_bias": ln1_bias,
            "wq_words": wq_words,
            "wq_scales": wq_scales,
            "bq": bq,
            "wk_words": wk_words,
            "wk_scales": wk_scales,
            "bk": bk,
            "wv_words": wv_words,
            "wv_scales": wv_scales,
            "bv": bv}


def reference(x, ln1_gain, ln1_bias, wq_words, wq_scales, bq, wk_words, wk_scales, bk, wv_words, wv_scales, bv):
    h = layer_norm(f64(x), f64(ln1_gain), f64(ln1_bias))
    hq = mxq(h, 2, "e4m3")
    q = ((hq @ unpack_weight(wq_words, wq_scales, FMT)) + f64(bq)).reshape(B, T, H, DH)
    k = ((hq @ unpack_weight(wk_words, wk_scales, FMT)) + f64(bk)).reshape(B, T, H, DH)
    v = ((hq @ unpack_weight(wv_words, wv_scales, FMT)) + f64(bv)).reshape(B, T, H, DH)
    return q, k, v

@@ -1,0 +1,203 @@
+from contextlib import ExitStack
+
+import concourse.mybir as mybir
+from concourse.masks import make_identity
+
+F32 = mybir.dt.float32
+BF16 = mybir.dt.bfloat16
+I32 = mybir.dt.int32
+U32 = mybir.dt.uint32
+U8 = mybir.dt.uint8
+FP8X4 = mybir.dt.float8_e4m3fn_x4
+ALU = mybir.AluOpType
+ACT = mybir.ActivationFunctionType
+
+P = 128
+PACK = 4
+K_PASS = P * PACK
+TOKENS = 4 * 1024
+K = 1024
+PASSES = K // K_PASS
+PLANES = PASSES * PACK
+WIDTH = 256
+OUTS = 3
+TILES = 2
+GROUP = TILES * P
+GROUPS = TOKENS // GROUP
+EPS = 1e-6
+BN_MAX = 512
+BN_CALLS = K // BN_MAX
+BN_DIM = 6
+LOAD_AHEAD = 2
+
+FLOPS = 2 * TOKENS * K * OUTS * WIDTH
+
+
+def tile_swidtblock_pa_t_kernel(
+    tc, x, ln1_gain, ln1_bias, wq_words, wq_scales, bq, wk_words, wk_scales, bk, wv_words, wv_scales, bv,
+    out_0, out_1, out_2,
+):
+    nc = tc.nc
+    x_groups = x.rearrange("b s k -> (b s) k").rearrange("(j q a) k -> j q a k", q=P, a=TILES)
+    out_groups = [
+        o.rearrange("b s h d -> (b s) (h d)").rearrange("(j q a) c -> j q a c", q=P, a=TILES)
+        for o in (out_0, out_1, out_2)
+    ]
+
+    with ExitStack() as ctx:
+        const = ctx.enter_context(tc.tile_pool(name="const", bufs=1))
+        x_pool = ctx.enter_context(tc.tile_pool(name="x_pool", bufs=6))
+        stat_pool = ctx.enter_context(tc.tile_pool(name="stat_pool", bufs=4))
+        n_pool = ctx.enter_context(tc.tile_pool(name="n_pool", bufs=4))
+        h_pool = ctx.enter_context(tc.tile_pool(name="h_pool", bufs=2))
+        o_pool = ctx.enter_context(tc.tile_pool(name="o_pool", bufs=3))
+        t_psum = ctx.enter_context(tc.psum_pool(name="t_psum", bufs=1))
+        acc_psum = ctx.enter_context(tc.psum_pool(name="acc_psum", bufs=2))
+
+        loaded = {}
+
+        def load(j):
+            x_sb = x_pool.tile([P, TILES, K], BF16)
+            nc.sync.dma_start(out=x_sb[:], in_=x_groups[j])
+            loaded[j] = x_sb
+
+        for j in range(LOAD_AHEAD):
+            load(j)
+
+        ident = const.tile([P, P], F32)
+        make_identity(nc, ident[:])
+        neg_half = const.tile([P, TILES], F32)
+        nc.gpsimd.memset(neg_half[:], -0.5)
+
+        gain_bf = const.tile([P, PASSES, PACK], BF16)
+        bias_bf = const.tile([P, PASSES, PACK], BF16)
+        nc.sync.dma_start(out=gain_bf[:], in_=ln1_gain.rearrange("(g p t) -> p g t", g=PASSES, p=P))
+        nc.sync.dma_start(out=bias_bf[:], in_=ln1_bias.rearrange("(g p t) -> p g t", g=PASSES, p=P))
+        gain_pt = const.tile([P, PLANES], F32)
+        bias_pt = const.tile([P, PLANES], F32)
+        nc.vector.tensor_copy(out=gain_pt[:], in_=gain_bf[:].rearrange("p g t -> p (g t)"))
+        nc.vector.tensor_copy(out=bias_pt[:], in_=bias_bf[:].rearrange("p g t -> p (g t)"))
+
+        w_codes = const.tile([P, PASSES, OUTS * WIDTH], U32, align_bytes=64)
+        w_scales = const.tile([P, PASSES, OUTS * WIDTH], U8, align_bytes=64)
+        nc.vector.memset(w_scales[:].rearrange("p g n -> p (g n)").bitcast(I32), 0)
+        for w, (words, scales) in enumerate(((wq_words, wq_scales), (wk_words, wk_scales), (wv_words, wv_scales))):
+            cols = slice(w * WIDTH, (w + 1) * WIDTH)
+            nc.sync.dma_start(
+                out=w_codes[:, :, cols].bitcast(I32),
+                in_=words.rearrange("g p n t -> p g (n t)").bitcast(I32),
+            )
+            for quad in range(4):
+                nc.sync.dma_start(
+                    out=w_scales[32 * quad : 32 * quad + 4, :, cols].bitcast(I32),
+                    in_=scales[:, 4 * quad : 4 * quad + 4, :].rearrange("g r n -> r g n").bitcast(I32),
+                )
+
+        b_bf = const.tile([P, OUTS, WIDTH], BF16)
+        for w, b in enumerate((bq, bk, bv)):
+            nc.sync.dma_start(out=b_bf[:, w, :], in_=b.partition_broadcast(P))
+        b_all = const.tile([P, OUTS, WIDTH], F32)
+        nc.vector.tensor_copy(out=b_all[:], in_=b_bf[:])
+
+        normed = {}
+        quantised_in = {}
+
+        def normalise(j):
+            x_sb = loaded[j]
+            stats = stat_pool.tile([P, TILES, BN_CALLS, BN_DIM], F32)
+            mean_var = stat_pool.tile([P, TILES, 2], F32)
+            for a in range(TILES):
+                for c in range(BN_CALLS):
+                    nc.vector.bn_stats(out=stats[:, a, c, :], in_=x_sb[:, a, c * BN_MAX : (c + 1) * BN_MAX])
+                nc.vector.bn_aggr(out=mean_var[:, a, :], in_=stats[:, a].rearrange("q c s -> q (c s)"))
+            neg_mean = stat_pool.tile([P, TILES], F32)
+            var_eps = stat_pool.tile([P, TILES], F32)
+            rstd = stat_pool.tile([P, TILES], F32)
+            nc.gpsimd.tensor_scalar(
+                out=neg_mean[:], in0=mean_var[:, :, 0], scalar1=-1.0, scalar2=0.0, op0=ALU.mult, op1=ALU.add
+            )
+            nc.gpsimd.tensor_scalar(
+                out=var_eps[:], in0=mean_var[:, :, 1], scalar1=1.0, scalar2=EPS, op0=ALU.mult, op1=ALU.add
+            )
+            nc.gpsimd.tensor_tensor(out=rstd[:], in0=var_eps[:], in1=neg_half[:], op=ALU.pow)
+            tiles = []
+            for a in range(TILES):
+                n_sb = n_pool.tile([P, PLANES, P], F32)
+                nc.gpsimd.tensor_scalar(
+                    out=n_sb[:].rearrange("q (g t) p -> q g t p", g=PASSES),
+                    in0=x_sb[:, a, :].rearrange("q (g p t) -> q g t p", g=PASSES, p=P),
+                    scalar1=neg_mean[:, a : a + 1],
+                    scalar2=rstd[:, a : a + 1],
+                    op0=ALU.add,
+                    op1=ALU.mult,
+                )
+                tiles.append(n_sb)
+            normed[j] = tiles
+
+        def turn(j):
+            planes = h_pool.tile([P, PLANES, GROUP], BF16)
+            for bank in range(PLANES // 2):
+                n_t = t_psum.tile([P, 2, GROUP], F32, name="n_t%d" % bank)
+                for half in range(2):
+                    for a in range(TILES):
+                        nc.tensor.transpose(
+                            n_t[:, half, a * P : (a + 1) * P], normed[j][a][:, 2 * bank + half, :], ident[:]
+                        )
+                for half in range(2):
+                    plane = 2 * bank + half
+                    nc.scalar.activation(
+                        out=planes[:, plane, :],
+                        in_=n_t[:, half, :],
+                        func=ACT.Identity,
+                        bias=bias_pt[:, plane : plane + 1],
+                        scale=gain_pt[:, plane : plane + 1],
+                    )
+            grouped = h_pool.tile([P, PASSES, GROUP, PACK], BF16, align_bytes=64)
+            for g in range(PASSES):
+                nc.scalar.copy(
+                    out=grouped[:, g].rearrange("p (c i) t -> p c t i", i=4),
+                    in_=planes[:, g * PACK : (g + 1) * PACK, :].rearrange("p t (c i) -> p c t i", i=4),
+                )
+            quantised_in[j] = grouped
+
+        def project(j):
+            h_codes = h_pool.tile([P, PASSES, GROUP], U32, align_bytes=64)
+            h_scales = h_pool.tile([P, PASSES, GROUP], U8, align_bytes=64)
+            nc.vector.quantize_mx(
+                out=h_codes[:].rearrange("p g c -> p (g c)").bitcast(FP8X4),
+                scales=h_scales[:].rearrange("p g c -> p (g c)"),
+                in_=quantised_in[j][:].rearrange("p g c t -> p (g c t)"),
+            )
+            o_sb = o_pool.tile([P, OUTS, TILES, WIDTH], F32)
+            acc_v = acc_psum.tile([P, TILES, WIDTH], F32)
+            for a in range(TILES):
+                toks = slice(a * P, (a + 1) * P)
+                acc_qk = acc_psum.tile([P, 2, WIDTH], F32)
+                for g in range(PASSES):
+                    for acc, cols in ((acc_qk[:].rearrange("q w c -> q (w c)"), slice(0, 2 * WIDTH)),
+                                      (acc_v[:, a, :], slice(2 * WIDTH, 3 * WIDTH))):
+                        nc.tensor.matmul_mx(
+                            out=acc,
+                            lhsT=h_codes[:, g, toks].bitcast(FP8X4),
+                            lhsT_scale=h_scales[:, g, toks],
+                            rhs=w_codes[:, g, cols].bitcast(FP8X4),
+                            rhs_scale=w_scales[:, g, cols],
+                            start=(g == 0),
+                            stop=(g == PASSES - 1),
+                        )
+                nc.vector.tensor_tensor(out=o_sb[:, 0:2, a, :], in0=acc_qk[:], in1=b_all[:, 0:2, :], op=ALU.add)
+            nc.vector.tensor_tensor(
+                out=o_sb[:, 2], in0=acc_v[:], in1=b_all[:, 2:3, :].to_broadcast([P, TILES, WIDTH]), op=ALU.add
+            )
+            for w in range(OUTS):
+                nc.sync.dma_start(out=out_groups[w][j], in_=o_sb[:, w])
+
+        for step in range(GROUPS + 2):
+            if step + LOAD_AHEAD < GROUPS:
+                load(step + LOAD_AHEAD)
+            if step < GROUPS:
+                normalise(step)
+            if 0 <= step - 1 < GROUPS:
+                turn(step - 1)
+            if 0 <= step - 2:
+                project(step - 2)

@@ -99,10 +99,13 @@ def tile_swidtblock_pa_t_kernel(
         b_all = const.tile([P, OUTS, WIDTH], F32)
         nc.vector.tensor_copy(out=b_all[:], in_=b_bf[:])
 
+        moments = {}
+        turned = {}
+        products = {}
         normed = {}
         quantised_in = {}
 
-        def normalise(j):
+        def statistics(j):
             x_sb = loaded[j]
             stats = stat_pool.tile([P, TILES, BN_CALLS, BN_DIM], F32)
             mean_var = stat_pool.tile([P, TILES, 2], F32)
@@ -110,6 +113,11 @@ def tile_swidtblock_pa_t_kernel(
                 for c in range(BN_CALLS):
                     nc.vector.bn_stats(out=stats[:, a, c, :], in_=x_sb[:, a, c * BN_MAX : (c + 1) * BN_MAX])
                 nc.vector.bn_aggr(out=mean_var[:, a, :], in_=stats[:, a].rearrange("q c s -> q (c s)"))
+            moments[j] = mean_var
+
+        def normalise(j):
+            x_sb = loaded[j]
+            mean_var = moments[j]
             neg_mean = stat_pool.tile([P, TILES], F32)
             var_eps = stat_pool.tile([P, TILES], F32)
             rstd = stat_pool.tile([P, TILES], F32)
@@ -152,6 +160,10 @@ def tile_swidtblock_pa_t_kernel(
                         bias=bias_pt[:, plane : plane + 1],
                         scale=gain_pt[:, plane : plane + 1],
                     )
+            turned[j] = planes
+
+        def regroup(j):
+            planes = turned[j]
             grouped = h_pool.tile([P, PASSES, GROUP, PACK], BF16, align_bytes=64)
             for g in range(PASSES):
                 nc.scalar.copy(
@@ -168,8 +180,8 @@ def tile_swidtblock_pa_t_kernel(
                 scales=h_scales[:].rearrange("p g c -> p (g c)"),
                 in_=quantised_in[j][:].rearrange("p g c t -> p (g c t)"),
             )
-            o_sb = o_pool.tile([P, OUTS, TILES, WIDTH], F32)
             acc_v = acc_psum.tile([P, TILES, WIDTH], F32)
+            accs_qk = []
             for a in range(TILES):
                 toks = slice(a * P, (a + 1) * P)
                 acc_qk = acc_psum.tile([P, 2, WIDTH], F32)
@@ -185,19 +197,33 @@ def tile_swidtblock_pa_t_kernel(
                             start=(g == 0),
                             stop=(g == PASSES - 1),
                         )
-                nc.vector.tensor_tensor(out=o_sb[:, 0:2, a, :], in0=acc_qk[:], in1=b_all[:, 0:2, :], op=ALU.add)
+                accs_qk.append(acc_qk)
+            products[j] = (accs_qk, acc_v)
+
+        def finish(j):
+            accs_qk, acc_v = products[j]
+            o_sb = o_pool.tile([P, OUTS, TILES, WIDTH], F32)
+            for a in range(TILES):
+                nc.vector.tensor_tensor(out=o_sb[:, 0:2, a, :], in0=accs_qk[a][:], in1=b_all[:, 0:2, :], op=ALU.add)
             nc.vector.tensor_tensor(
                 out=o_sb[:, 2], in0=acc_v[:], in1=b_all[:, 2:3, :].to_broadcast([P, TILES, WIDTH]), op=ALU.add
             )
             for w in range(OUTS):
                 nc.sync.dma_start(out=out_groups[w][j], in_=o_sb[:, w])
 
-        for step in range(GROUPS + 2):
-            if step + LOAD_AHEAD < GROUPS:
-                load(step + LOAD_AHEAD)
-            if step < GROUPS:
-                normalise(step)
-            if 0 <= step - 1 < GROUPS:
-                turn(step - 1)
-            if 0 <= step - 2:
-                project(step - 2)
+        with tc.manual_schedule():
+            for step in range(GROUPS + 3):
+                if step + LOAD_AHEAD < GROUPS:
+                    load(step + LOAD_AHEAD)
+                if 0 <= step - 2 < GROUPS:
+                    turn(step - 2)
+                if 0 <= step - 3:
+                    project(step - 3)
+                if step < GROUPS:
+                    statistics(step)
+                if 0 <= step - 1 < GROUPS:
+                    normalise(step - 1)
+                if 0 <= step - 2 < GROUPS:
+                    regroup(step - 2)
+                if 0 <= step - 3:
+                    finish(step - 3)

@@ -29,6 +29,7 @@ BN_MAX = 512
 BN_CALLS = K // BN_MAX
 BN_DIM = 6
 LOAD_AHEAD = 2
+AHEAD = 3
 
 FLOPS = 2 * TOKENS * K * OUTS * WIDTH
 
@@ -48,7 +49,7 @@ def tile_swidtblock_pa_t_kernel(
         const = ctx.enter_context(tc.tile_pool(name="const", bufs=1))
         x_pool = ctx.enter_context(tc.tile_pool(name="x_pool", bufs=6))
         stat_pool = ctx.enter_context(tc.tile_pool(name="stat_pool", bufs=4))
-        n_pool = ctx.enter_context(tc.tile_pool(name="n_pool", bufs=4))
+        n_pool = ctx.enter_context(tc.tile_pool(name="n_pool", bufs=TILES * AHEAD))
         h_pool = ctx.enter_context(tc.tile_pool(name="h_pool", bufs=2))
         o_pool = ctx.enter_context(tc.tile_pool(name="o_pool", bufs=3))
         t_psum = ctx.enter_context(tc.psum_pool(name="t_psum", bufs=1))
@@ -99,8 +100,10 @@ def tile_swidtblock_pa_t_kernel(
         b_all = const.tile([P, OUTS, WIDTH], F32)
         nc.vector.tensor_copy(out=b_all[:], in_=b_bf[:])
 
+        partial = {}
         moments = {}
         turned = {}
+        quantised = {}
         products = {}
         normed = {}
         quantised_in = {}
@@ -108,11 +111,15 @@ def tile_swidtblock_pa_t_kernel(
         def statistics(j):
             x_sb = loaded[j]
             stats = stat_pool.tile([P, TILES, BN_CALLS, BN_DIM], F32)
-            mean_var = stat_pool.tile([P, TILES, 2], F32)
             for a in range(TILES):
                 for c in range(BN_CALLS):
                     nc.vector.bn_stats(out=stats[:, a, c, :], in_=x_sb[:, a, c * BN_MAX : (c + 1) * BN_MAX])
-                nc.vector.bn_aggr(out=mean_var[:, a, :], in_=stats[:, a].rearrange("q c s -> q (c s)"))
+            partial[j] = stats
+
+        def aggregate(j):
+            mean_var = stat_pool.tile([P, TILES, 2], F32)
+            for a in range(TILES):
+                nc.vector.bn_aggr(out=mean_var[:, a, :], in_=partial[j][:, a].rearrange("q c s -> q (c s)"))
             moments[j] = mean_var
 
         def normalise(j):
@@ -172,7 +179,7 @@ def tile_swidtblock_pa_t_kernel(
                 )
             quantised_in[j] = grouped
 
-        def project(j):
+        def quantise(j):
             h_codes = h_pool.tile([P, PASSES, GROUP], U32, align_bytes=64)
             h_scales = h_pool.tile([P, PASSES, GROUP], U8, align_bytes=64)
             nc.vector.quantize_mx(
@@ -180,6 +187,10 @@ def tile_swidtblock_pa_t_kernel(
                 scales=h_scales[:].rearrange("p g c -> p (g c)"),
                 in_=quantised_in[j][:].rearrange("p g c t -> p (g c t)"),
             )
+            quantised[j] = (h_codes, h_scales)
+
+        def multiply(j):
+            h_codes, h_scales = quantised[j]
             acc_v = acc_psum.tile([P, TILES, WIDTH], F32)
             accs_qk = []
             for a in range(TILES):
@@ -212,18 +223,22 @@ def tile_swidtblock_pa_t_kernel(
                 nc.sync.dma_start(out=out_groups[w][j], in_=o_sb[:, w])
 
         with tc.manual_schedule():
-            for step in range(GROUPS + 3):
+            for step in range(GROUPS + AHEAD + 2):
                 if step + LOAD_AHEAD < GROUPS:
                     load(step + LOAD_AHEAD)
-                if 0 <= step - 2 < GROUPS:
-                    turn(step - 2)
-                if 0 <= step - 3:
-                    project(step - 3)
+                if 0 <= step - AHEAD < GROUPS:
+                    turn(step - AHEAD)
+                if 0 <= step - AHEAD - 2:
+                    multiply(step - AHEAD - 2)
+                if 0 <= step - AHEAD - 1 < GROUPS:
+                    quantise(step - AHEAD - 1)
                 if step < GROUPS:
                     statistics(step)
                 if 0 <= step - 1 < GROUPS:
                     normalise(step - 1)
-                if 0 <= step - 2 < GROUPS:
-                    regroup(step - 2)
-                if 0 <= step - 3:
-                    finish(step - 3)
+                if 0 <= step - AHEAD < GROUPS:
+                    regroup(step - AHEAD)
+                if 0 <= step - AHEAD - 2:
+                    finish(step - AHEAD - 2)
+                if step < GROUPS:
+                    aggregate(step)

@@ -28,7 +28,7 @@ EPS = 1e-6
 BN_MAX = 512
 BN_CALLS = K // BN_MAX
 BN_DIM = 6
-LOAD_AHEAD = 2
+LOAD_AHEAD = 5
 AHEAD = 3
 
 FLOPS = 2 * TOKENS * K * OUTS * WIDTH
@@ -47,7 +47,7 @@ def tile_swidtblock_pa_t_kernel(
 
     with ExitStack() as ctx:
         const = ctx.enter_context(tc.tile_pool(name="const", bufs=1))
-        x_pool = ctx.enter_context(tc.tile_pool(name="x_pool", bufs=6))
+        x_pool = ctx.enter_context(tc.tile_pool(name="x_pool", bufs=LOAD_AHEAD + 3))
         stat_pool = ctx.enter_context(tc.tile_pool(name="stat_pool", bufs=4))
         n_pool = ctx.enter_context(tc.tile_pool(name="n_pool", bufs=TILES * AHEAD))
         h_pool = ctx.enter_context(tc.tile_pool(name="h_pool", bufs=2))

@@ -62,7 +62,12 @@ def tile_swidtblock_pa_t_kernel(
             nc.sync.dma_start(out=x_sb[:], in_=x_groups[j])
             loaded[j] = x_sb
 
-        for j in range(LOAD_AHEAD):
+        load(0)
+        gain_bf = const.tile([P, PASSES, PACK], BF16)
+        bias_bf = const.tile([P, PASSES, PACK], BF16)
+        nc.sync.dma_start(out=gain_bf[:], in_=ln1_gain.rearrange("(g p t) -> p g t", g=PASSES, p=P))
+        nc.sync.dma_start(out=bias_bf[:], in_=ln1_bias.rearrange("(g p t) -> p g t", g=PASSES, p=P))
+        for j in range(1, LOAD_AHEAD):
             load(j)
 
         ident = const.tile([P, P], F32)
@@ -70,10 +75,6 @@ def tile_swidtblock_pa_t_kernel(
         neg_half = const.tile([P, TILES], F32)
         nc.gpsimd.memset(neg_half[:], -0.5)
 
-        gain_bf = const.tile([P, PASSES, PACK], BF16)
-        bias_bf = const.tile([P, PASSES, PACK], BF16)
-        nc.sync.dma_start(out=gain_bf[:], in_=ln1_gain.rearrange("(g p t) -> p g t", g=PASSES, p=P))
-        nc.sync.dma_start(out=bias_bf[:], in_=ln1_bias.rearrange("(g p t) -> p g t", g=PASSES, p=P))
         gain_pt = const.tile([P, PLANES], F32)
         bias_pt = const.tile([P, PLANES], F32)
         nc.vector.tensor_copy(out=gain_pt[:], in_=gain_bf[:].rearrange("p g t -> p (g t)"))
@@ -215,9 +216,9 @@ def tile_swidtblock_pa_t_kernel(
             accs_qk, acc_v = products[j]
             o_sb = o_pool.tile([P, OUTS, TILES, WIDTH], F32)
             for a in range(TILES):
-                nc.vector.tensor_tensor(out=o_sb[:, 0:2, a, :], in0=accs_qk[a][:], in1=b_all[:, 0:2, :], op=ALU.add)
+                nc.vector.tensor_tensor(out=o_sb[:, 0:2, a, :], in0=b_all[:, 0:2, :], in1=accs_qk[a][:], op=ALU.add)
             nc.vector.tensor_tensor(
-                out=o_sb[:, 2], in0=acc_v[:], in1=b_all[:, 2:3, :].to_broadcast([P, TILES, WIDTH]), op=ALU.add
+                out=o_sb[:, 2], in0=b_all[:, 2:3, :].to_broadcast([P, TILES, WIDTH]), in1=acc_v[:], op=ALU.add
             )
             for w in range(OUTS):
                 nc.sync.dma_start(out=out_groups[w][j], in_=o_sb[:, w])

@@ -72,8 +72,6 @@ def tile_swidtblock_pa_t_kernel(
 
         ident = const.tile([P, P], F32)
         make_identity(nc, ident[:])
-        neg_half = const.tile([P, TILES], F32)
-        nc.gpsimd.memset(neg_half[:], -0.5)
 
         gain_pt = const.tile([P, PLANES], F32)
         bias_pt = const.tile([P, PLANES], F32)
@@ -108,6 +106,7 @@ def tile_swidtblock_pa_t_kernel(
         products = {}
         normed = {}
         quantised_in = {}
+        factors = {}
 
         def statistics(j):
             x_sb = loaded[j]
@@ -123,19 +122,18 @@ def tile_swidtblock_pa_t_kernel(
                 nc.vector.bn_aggr(out=mean_var[:, a, :], in_=partial[j][:, a].rearrange("q c s -> q (c s)"))
             moments[j] = mean_var
 
+        def root(j):
+            rstd = stat_pool.tile([P, TILES], F32)
+            neg_mean = stat_pool.tile([P, TILES], F32)
+            nc.scalar.activation(
+                out=rstd[:], in_=moments[j][:, :, 1], func=ACT.Abs_reciprocal_sqrt, bias=EPS, scale=1.0
+            )
+            nc.scalar.activation(out=neg_mean[:], in_=moments[j][:, :, 0], func=ACT.Copy, scale=-1.0)
+            factors[j] = (neg_mean, rstd)
+
         def normalise(j):
             x_sb = loaded[j]
-            mean_var = moments[j]
-            neg_mean = stat_pool.tile([P, TILES], F32)
-            var_eps = stat_pool.tile([P, TILES], F32)
-            rstd = stat_pool.tile([P, TILES], F32)
-            nc.gpsimd.tensor_scalar(
-                out=neg_mean[:], in0=mean_var[:, :, 0], scalar1=-1.0, scalar2=0.0, op0=ALU.mult, op1=ALU.add
-            )
-            nc.gpsimd.tensor_scalar(
-                out=var_eps[:], in0=mean_var[:, :, 1], scalar1=1.0, scalar2=EPS, op0=ALU.mult, op1=ALU.add
-            )
-            nc.gpsimd.tensor_tensor(out=rstd[:], in0=var_eps[:], in1=neg_half[:], op=ALU.pow)
+            neg_mean, rstd = factors[j]
             tiles = []
             for a in range(TILES):
                 n_sb = n_pool.tile([P, PLANES, P], F32)
@@ -173,11 +171,22 @@ def tile_swidtblock_pa_t_kernel(
         def regroup(j):
             planes = turned[j]
             grouped = h_pool.tile([P, PASSES, GROUP, PACK], BF16, align_bytes=64)
-            for g in range(PASSES):
-                nc.scalar.copy(
-                    out=grouped[:, g].rearrange("p (c i) t -> p c t i", i=4),
-                    in_=planes[:, g * PACK : (g + 1) * PACK, :].rearrange("p t (c i) -> p c t i", i=4),
-                )
+            nc.scalar.copy(
+                out=grouped[:, 0].rearrange("p (c i) t -> p c t i", i=4),
+                in_=planes[:, 0:PACK, :].rearrange("p t (c i) -> p c t i", i=4),
+            )
+            nc.scalar.copy(
+                out=grouped[:, 1, 0:P, :].rearrange("p (c i) t -> p c t i", i=4),
+                in_=planes[:, PACK : 2 * PACK, 0:P].rearrange("p t (c i) -> p c t i", i=4),
+            )
+            nc.gpsimd.tensor_scalar(
+                out=grouped[:, 1, P:GROUP, :],
+                in0=planes[:, PACK : 2 * PACK, P:GROUP].rearrange("p t c -> p c t"),
+                scalar1=1.0,
+                scalar2=0.0,
+                op0=ALU.mult,
+                op1=ALU.add,
+            )
             quantised_in[j] = grouped
 
         def quantise(j):
@@ -229,6 +238,8 @@ def tile_swidtblock_pa_t_kernel(
                     load(step + LOAD_AHEAD)
                 if 0 <= step - AHEAD < GROUPS:
                     turn(step - AHEAD)
+                if 0 <= step - 1 < GROUPS:
+                    root(step - 1)
                 if 0 <= step - AHEAD - 2:
                     multiply(step - AHEAD - 2)
                 if 0 <= step - AHEAD - 1 < GROUPS:

@@ -107,6 +107,11 @@ def tile_swidtblock_pa_t_kernel(
         normed = {}
         quantised_in = {}
         factors = {}
+        shifts = {}
+        last_bank = {}
+
+        def late(j):
+            return j >= GROUPS - 2
 
         def statistics(j):
             x_sb = loaded[j]
@@ -130,6 +135,13 @@ def tile_swidtblock_pa_t_kernel(
             )
             nc.scalar.activation(out=neg_mean[:], in_=moments[j][:, :, 0], func=ACT.Copy, scale=-1.0)
             factors[j] = (neg_mean, rstd)
+            if j == 0:
+                a = TILES - 1
+                shift = stat_pool.tile([P, 1], F32)
+                nc.scalar.activation(
+                    out=shift[:], in_=neg_mean[:, a : a + 1], func=ACT.Copy, scale=rstd[:, a : a + 1]
+                )
+                shifts[j] = shift
 
         def normalise(j):
             x_sb = loaded[j]
@@ -137,14 +149,23 @@ def tile_swidtblock_pa_t_kernel(
             tiles = []
             for a in range(TILES):
                 n_sb = n_pool.tile([P, PLANES, P], F32)
-                nc.gpsimd.tensor_scalar(
-                    out=n_sb[:].rearrange("q (g t) p -> q g t p", g=PASSES),
-                    in0=x_sb[:, a, :].rearrange("q (g p t) -> q g t p", g=PASSES, p=P),
-                    scalar1=neg_mean[:, a : a + 1],
-                    scalar2=rstd[:, a : a + 1],
-                    op0=ALU.add,
-                    op1=ALU.mult,
-                )
+                if j == 0 and a == TILES - 1:
+                    nc.scalar.activation(
+                        out=n_sb[:].rearrange("q (g t) p -> q g t p", g=PASSES),
+                        in_=x_sb[:, a, :].rearrange("q (g p t) -> q g t p", g=PASSES, p=P),
+                        func=ACT.Identity,
+                        bias=shifts[j][:],
+                        scale=rstd[:, a : a + 1],
+                    )
+                else:
+                    nc.gpsimd.tensor_scalar(
+                        out=n_sb[:].rearrange("q (g t) p -> q g t p", g=PASSES),
+                        in0=x_sb[:, a, :].rearrange("q (g p t) -> q g t p", g=PASSES, p=P),
+                        scalar1=neg_mean[:, a : a + 1],
+                        scalar2=rstd[:, a : a + 1],
+                        op0=ALU.add,
+                        op1=ALU.mult,
+                    )
                 tiles.append(n_sb)
             normed[j] = tiles
 
@@ -157,16 +178,31 @@ def tile_swidtblock_pa_t_kernel(
                         nc.tensor.transpose(
                             n_t[:, half, a * P : (a + 1) * P], normed[j][a][:, 2 * bank + half, :], ident[:]
                         )
-                for half in range(2):
-                    plane = 2 * bank + half
-                    nc.scalar.activation(
-                        out=planes[:, plane, :],
-                        in_=n_t[:, half, :],
-                        func=ACT.Identity,
-                        bias=bias_pt[:, plane : plane + 1],
-                        scale=gain_pt[:, plane : plane + 1],
-                    )
+                if late(j) and bank == PLANES // 2 - 1:
+                    last_bank[j] = n_t
+                else:
+                    for half in range(2):
+                        plane = 2 * bank + half
+                        nc.scalar.activation(
+                            out=planes[:, plane, :],
+                            in_=n_t[:, half, :],
+                            func=ACT.Identity,
+                            bias=bias_pt[:, plane : plane + 1],
+                            scale=gain_pt[:, plane : plane + 1],
+                        )
             turned[j] = planes
+
+        def turn_last(j):
+            for half in range(2):
+                plane = PLANES - 2 + half
+                nc.vector.tensor_scalar(
+                    out=turned[j][:, plane, :],
+                    in0=last_bank[j][:, half, :],
+                    scalar1=gain_pt[:, plane : plane + 1],
+                    scalar2=bias_pt[:, plane : plane + 1],
+                    op0=ALU.mult,
+                    op1=ALU.add,
+                )
 
         def regroup(j):
             planes = turned[j]
@@ -175,13 +211,15 @@ def tile_swidtblock_pa_t_kernel(
                 out=grouped[:, 0].rearrange("p (c i) t -> p c t i", i=4),
                 in_=planes[:, 0:PACK, :].rearrange("p t (c i) -> p c t i", i=4),
             )
-            nc.scalar.copy(
-                out=grouped[:, 1, 0:P, :].rearrange("p (c i) t -> p c t i", i=4),
-                in_=planes[:, PACK : 2 * PACK, 0:P].rearrange("p t (c i) -> p c t i", i=4),
-            )
+            first = 0 if late(j) else P
+            if first > 0:
+                nc.scalar.copy(
+                    out=grouped[:, 1, 0:first, :].rearrange("p (c i) t -> p c t i", i=4),
+                    in_=planes[:, PACK : 2 * PACK, 0:first].rearrange("p t (c i) -> p c t i", i=4),
+                )
             nc.gpsimd.tensor_scalar(
-                out=grouped[:, 1, P:GROUP, :],
-                in0=planes[:, PACK : 2 * PACK, P:GROUP].rearrange("p t c -> p c t"),
+                out=grouped[:, 1, first:GROUP, :],
+                in0=planes[:, PACK : 2 * PACK, first:GROUP].rearrange("p t c -> p c t"),
                 scalar1=1.0,
                 scalar2=0.0,
                 op0=ALU.mult,
@@ -246,10 +284,12 @@ def tile_swidtblock_pa_t_kernel(
                     quantise(step - AHEAD - 1)
                 if step < GROUPS:
                     statistics(step)
-                if 0 <= step - 1 < GROUPS:
-                    normalise(step - 1)
+                if 0 <= step - AHEAD < GROUPS and late(step - AHEAD):
+                    turn_last(step - AHEAD)
                 if 0 <= step - AHEAD < GROUPS:
                     regroup(step - AHEAD)
+                if 0 <= step - 1 < GROUPS:
+                    normalise(step - 1)
                 if 0 <= step - AHEAD - 2:
                     finish(step - AHEAD - 2)
                 if step < GROUPS:

@@ -22,8 +22,10 @@ PLANES = PASSES * PACK
 WIDTH = 256
 OUTS = 3
 TILES = 2
-GROUP = TILES * P
-GROUPS = TOKENS // GROUP
+SHORT = 2
+SIZES = [1] * SHORT + [TILES] * (TOKENS // (TILES * P) - SHORT) + [1] * SHORT
+GROUPS = len(SIZES)
+STARTS = [P * sum(SIZES[:j]) for j in range(GROUPS)]
 EPS = 1e-6
 BN_MAX = 512
 BN_CALLS = K // BN_MAX
@@ -39,11 +41,11 @@ def tile_swidtblock_pa_t_kernel(
     out_0, out_1, out_2,
 ):
     nc = tc.nc
-    x_groups = x.rearrange("b s k -> (b s) k").rearrange("(j q a) k -> j q a k", q=P, a=TILES)
-    out_groups = [
-        o.rearrange("b s h d -> (b s) (h d)").rearrange("(j q a) c -> j q a c", q=P, a=TILES)
-        for o in (out_0, out_1, out_2)
-    ]
+    x_tokens = x.rearrange("b s k -> (b s) k")
+    out_tokens = [o.rearrange("b s h d -> (b s) (h d)") for o in (out_0, out_1, out_2)]
+
+    def group_rows(rows, j):
+        return rows[STARTS[j] : STARTS[j] + SIZES[j] * P].rearrange("(q a) c -> q a c", a=SIZES[j])
 
     with ExitStack() as ctx:
         const = ctx.enter_context(tc.tile_pool(name="const", bufs=1))
@@ -58,8 +60,8 @@ def tile_swidtblock_pa_t_kernel(
         loaded = {}
 
         def load(j):
-            x_sb = x_pool.tile([P, TILES, K], BF16)
-            nc.sync.dma_start(out=x_sb[:], in_=x_groups[j])
+            x_sb = x_pool.tile([P, SIZES[j], K], BF16)
+            nc.sync.dma_start(out=x_sb[:], in_=group_rows(x_tokens, j))
             loaded[j] = x_sb
 
         load(0)
@@ -111,45 +113,48 @@ def tile_swidtblock_pa_t_kernel(
         last_bank = {}
 
         def late(j):
-            return j >= GROUPS - 2
+            return j == GROUPS - 1
+
+        def on_scalar(j, a):
+            return j == SHORT and a == TILES - 1
 
         def statistics(j):
             x_sb = loaded[j]
-            stats = stat_pool.tile([P, TILES, BN_CALLS, BN_DIM], F32)
-            for a in range(TILES):
+            stats = stat_pool.tile([P, SIZES[j], BN_CALLS, BN_DIM], F32)
+            for a in range(SIZES[j]):
                 for c in range(BN_CALLS):
                     nc.vector.bn_stats(out=stats[:, a, c, :], in_=x_sb[:, a, c * BN_MAX : (c + 1) * BN_MAX])
             partial[j] = stats
 
         def aggregate(j):
-            mean_var = stat_pool.tile([P, TILES, 2], F32)
-            for a in range(TILES):
+            mean_var = stat_pool.tile([P, SIZES[j], 2], F32)
+            for a in range(SIZES[j]):
                 nc.vector.bn_aggr(out=mean_var[:, a, :], in_=partial[j][:, a].rearrange("q c s -> q (c s)"))
             moments[j] = mean_var
 
         def root(j):
-            rstd = stat_pool.tile([P, TILES], F32)
-            neg_mean = stat_pool.tile([P, TILES], F32)
+            rstd = stat_pool.tile([P, SIZES[j]], F32)
+            neg_mean = stat_pool.tile([P, SIZES[j]], F32)
             nc.scalar.activation(
                 out=rstd[:], in_=moments[j][:, :, 1], func=ACT.Abs_reciprocal_sqrt, bias=EPS, scale=1.0
             )
             nc.scalar.activation(out=neg_mean[:], in_=moments[j][:, :, 0], func=ACT.Copy, scale=-1.0)
             factors[j] = (neg_mean, rstd)
-            if j == 0:
-                a = TILES - 1
-                shift = stat_pool.tile([P, 1], F32)
-                nc.scalar.activation(
-                    out=shift[:], in_=neg_mean[:, a : a + 1], func=ACT.Copy, scale=rstd[:, a : a + 1]
-                )
-                shifts[j] = shift
+            for a in range(SIZES[j]):
+                if on_scalar(j, a):
+                    shift = stat_pool.tile([P, 1], F32)
+                    nc.scalar.activation(
+                        out=shift[:], in_=neg_mean[:, a : a + 1], func=ACT.Copy, scale=rstd[:, a : a + 1]
+                    )
+                    shifts[j] = shift
 
         def normalise(j):
             x_sb = loaded[j]
             neg_mean, rstd = factors[j]
             tiles = []
-            for a in range(TILES):
+            for a in range(SIZES[j]):
                 n_sb = n_pool.tile([P, PLANES, P], F32)
-                if j == 0 and a == TILES - 1:
+                if on_scalar(j, a):
                     nc.scalar.activation(
                         out=n_sb[:].rearrange("q (g t) p -> q g t p", g=PASSES),
                         in_=x_sb[:, a, :].rearrange("q (g p t) -> q g t p", g=PASSES, p=P),
@@ -170,11 +175,11 @@ def tile_swidtblock_pa_t_kernel(
             normed[j] = tiles
 
         def turn(j):
-            planes = h_pool.tile([P, PLANES, GROUP], BF16)
+            planes = h_pool.tile([P, PLANES, SIZES[j] * P], BF16)
             for bank in range(PLANES // 2):
-                n_t = t_psum.tile([P, 2, GROUP], F32, name="n_t%d" % bank)
+                n_t = t_psum.tile([P, 2, SIZES[j] * P], F32, name="n_t%d" % bank)
                 for half in range(2):
-                    for a in range(TILES):
+                    for a in range(SIZES[j]):
                         nc.tensor.transpose(
                             n_t[:, half, a * P : (a + 1) * P], normed[j][a][:, 2 * bank + half, :], ident[:]
                         )
@@ -206,20 +211,21 @@ def tile_swidtblock_pa_t_kernel(
 
         def regroup(j):
             planes = turned[j]
-            grouped = h_pool.tile([P, PASSES, GROUP, PACK], BF16, align_bytes=64)
+            tokens = SIZES[j] * P
+            grouped = h_pool.tile([P, PASSES, tokens, PACK], BF16, align_bytes=64)
             nc.scalar.copy(
                 out=grouped[:, 0].rearrange("p (c i) t -> p c t i", i=4),
                 in_=planes[:, 0:PACK, :].rearrange("p t (c i) -> p c t i", i=4),
             )
-            first = 0 if late(j) else P
+            first = 0 if late(j) else tokens // 2
             if first > 0:
                 nc.scalar.copy(
                     out=grouped[:, 1, 0:first, :].rearrange("p (c i) t -> p c t i", i=4),
                     in_=planes[:, PACK : 2 * PACK, 0:first].rearrange("p t (c i) -> p c t i", i=4),
                 )
             nc.gpsimd.tensor_scalar(
-                out=grouped[:, 1, first:GROUP, :],
-                in0=planes[:, PACK : 2 * PACK, first:GROUP].rearrange("p t c -> p c t"),
+                out=grouped[:, 1, first:tokens, :],
+                in0=planes[:, PACK : 2 * PACK, first:tokens].rearrange("p t c -> p c t"),
                 scalar1=1.0,
                 scalar2=0.0,
                 op0=ALU.mult,
@@ -228,8 +234,8 @@ def tile_swidtblock_pa_t_kernel(
             quantised_in[j] = grouped
 
         def quantise(j):
-            h_codes = h_pool.tile([P, PASSES, GROUP], U32, align_bytes=64)
-            h_scales = h_pool.tile([P, PASSES, GROUP], U8, align_bytes=64)
+            h_codes = h_pool.tile([P, PASSES, SIZES[j] * P], U32, align_bytes=64)
+            h_scales = h_pool.tile([P, PASSES, SIZES[j] * P], U8, align_bytes=64)
             nc.vector.quantize_mx(
                 out=h_codes[:].rearrange("p g c -> p (g c)").bitcast(FP8X4),
                 scales=h_scales[:].rearrange("p g c -> p (g c)"),
@@ -239,9 +245,9 @@ def tile_swidtblock_pa_t_kernel(
 
         def multiply(j):
             h_codes, h_scales = quantised[j]
-            acc_v = acc_psum.tile([P, TILES, WIDTH], F32)
+            acc_v = acc_psum.tile([P, SIZES[j], WIDTH], F32)
             accs_qk = []
-            for a in range(TILES):
+            for a in range(SIZES[j]):
                 toks = slice(a * P, (a + 1) * P)
                 acc_qk = acc_psum.tile([P, 2, WIDTH], F32)
                 for g in range(PASSES):
@@ -261,14 +267,14 @@ def tile_swidtblock_pa_t_kernel(
 
         def finish(j):
             accs_qk, acc_v = products[j]
-            o_sb = o_pool.tile([P, OUTS, TILES, WIDTH], F32)
-            for a in range(TILES):
+            o_sb = o_pool.tile([P, OUTS, SIZES[j], WIDTH], F32)
+            for a in range(SIZES[j]):
                 nc.vector.tensor_tensor(out=o_sb[:, 0:2, a, :], in0=b_all[:, 0:2, :], in1=accs_qk[a][:], op=ALU.add)
             nc.vector.tensor_tensor(
-                out=o_sb[:, 2], in0=b_all[:, 2:3, :].to_broadcast([P, TILES, WIDTH]), in1=acc_v[:], op=ALU.add
+                out=o_sb[:, 2], in0=b_all[:, 2:3, :].to_broadcast([P, SIZES[j], WIDTH]), in1=acc_v[:], op=ALU.add
             )
             for w in range(OUTS):
-                nc.sync.dma_start(out=out_groups[w][j], in_=o_sb[:, w])
+                nc.sync.dma_start(out=group_rows(out_tokens[w], j), in_=o_sb[:, w])
 
         with tc.manual_schedule():
             for step in range(GROUPS + AHEAD + 2):

@@ -51,9 +51,9 @@ def tile_swidtblock_pa_t_kernel(
         const = ctx.enter_context(tc.tile_pool(name="const", bufs=1))
         x_pool = ctx.enter_context(tc.tile_pool(name="x_pool", bufs=LOAD_AHEAD + 3))
         stat_pool = ctx.enter_context(tc.tile_pool(name="stat_pool", bufs=4))
-        n_pool = ctx.enter_context(tc.tile_pool(name="n_pool", bufs=TILES * AHEAD))
-        h_pool = ctx.enter_context(tc.tile_pool(name="h_pool", bufs=2))
-        o_pool = ctx.enter_context(tc.tile_pool(name="o_pool", bufs=3))
+        n_pool = ctx.enter_context(tc.tile_pool(name="n_pool", bufs=TILES * (AHEAD + 1)))
+        h_pool = ctx.enter_context(tc.tile_pool(name="h_pool", bufs=3))
+        o_pool = ctx.enter_context(tc.tile_pool(name="o_pool", bufs=4))
         t_psum = ctx.enter_context(tc.psum_pool(name="t_psum", bufs=1))
         acc_psum = ctx.enter_context(tc.psum_pool(name="acc_psum", bufs=2))
 
@@ -61,7 +61,12 @@ def tile_swidtblock_pa_t_kernel(
 
         def load(j):
             x_sb = x_pool.tile([P, SIZES[j], K], BF16)
-            nc.sync.dma_start(out=x_sb[:], in_=group_rows(x_tokens, j))
+            if j == 0:
+                for c in range(BN_CALLS):
+                    cols = slice(c * BN_MAX, (c + 1) * BN_MAX)
+                    nc.sync.dma_start(out=x_sb[:, :, cols], in_=group_rows(x_tokens, j)[:, :, cols])
+            else:
+                nc.sync.dma_start(out=x_sb[:], in_=group_rows(x_tokens, j))
             loaded[j] = x_sb
 
         load(0)

@@ -31,6 +31,7 @@ BN_MAX = 512
 BN_CALLS = K // BN_MAX
 BN_DIM = 6
 LOAD_AHEAD = 5
+SCALAR_STATS = 12
 AHEAD = 3
 
 FLOPS = 2 * TOKENS * K * OUTS * WIDTH
@@ -53,6 +54,7 @@ def tile_swidtblock_pa_t_kernel(
         stat_pool = ctx.enter_context(tc.tile_pool(name="stat_pool", bufs=4))
         n_pool = ctx.enter_context(tc.tile_pool(name="n_pool", bufs=TILES * (AHEAD + 1)))
         h_pool = ctx.enter_context(tc.tile_pool(name="h_pool", bufs=3))
+        scratch_pool = ctx.enter_context(tc.tile_pool(name="scratch_pool", bufs=2))
         o_pool = ctx.enter_context(tc.tile_pool(name="o_pool", bufs=4))
         t_psum = ctx.enter_context(tc.psum_pool(name="t_psum", bufs=1))
         acc_psum = ctx.enter_context(tc.psum_pool(name="acc_psum", bufs=2))
@@ -120,31 +122,63 @@ def tile_swidtblock_pa_t_kernel(
         def late(j):
             return j == GROUPS - 1
 
+        def vector_tiles(j):
+            return SIZES[j] - 1 if j == SCALAR_STATS else SIZES[j]
+
         def on_scalar(j, a):
             return j == SHORT and a == TILES - 1
 
         def statistics(j):
             x_sb = loaded[j]
             stats = stat_pool.tile([P, SIZES[j], BN_CALLS, BN_DIM], F32)
-            for a in range(SIZES[j]):
+            for a in range(vector_tiles(j)):
                 for c in range(BN_CALLS):
                     nc.vector.bn_stats(out=stats[:, a, c, :], in_=x_sb[:, a, c * BN_MAX : (c + 1) * BN_MAX])
             partial[j] = stats
 
         def aggregate(j):
             mean_var = stat_pool.tile([P, SIZES[j], 2], F32)
-            for a in range(SIZES[j]):
+            for a in range(vector_tiles(j)):
                 nc.vector.bn_aggr(out=mean_var[:, a, :], in_=partial[j][:, a].rearrange("q c s -> q (c s)"))
             moments[j] = mean_var
 
-        def root(j):
-            rstd = stat_pool.tile([P, SIZES[j]], F32)
-            neg_mean = stat_pool.tile([P, SIZES[j]], F32)
-            nc.scalar.activation(
-                out=rstd[:], in_=moments[j][:, :, 1], func=ACT.Abs_reciprocal_sqrt, bias=EPS, scale=1.0
-            )
-            nc.scalar.activation(out=neg_mean[:], in_=moments[j][:, :, 0], func=ACT.Copy, scale=-1.0)
+        def scalar_sum(j):
+            a = SIZES[j] - 1
+            neg_mean = stat_pool.tile([P, SIZES[j]], F32, name="neg_mean")
+            rstd = stat_pool.tile([P, SIZES[j]], F32, name="rstd")
             factors[j] = (neg_mean, rstd)
+            total = stat_pool.tile([P, 1], F32)
+            scratch = scratch_pool.tile([P, K], BF16)
+            nc.scalar.activation(out=scratch[:], in_=loaded[j][:, a, :], func=ACT.Identity, accum_out=total[:])
+            nc.scalar.activation(out=neg_mean[:, a : a + 1], in_=total[:], func=ACT.Copy, scale=-1.0 / K)
+
+        def scalar_square(j):
+            a = SIZES[j] - 1
+            neg_mean, rstd = factors[j]
+            squares = stat_pool.tile([P, 1], F32)
+            scratch = scratch_pool.tile([P, K], BF16)
+            nc.scalar.activation(
+                out=scratch[:],
+                in_=loaded[j][:, a, :],
+                func=ACT.Square,
+                bias=neg_mean[:, a : a + 1],
+                accum_out=squares[:],
+            )
+            nc.scalar.activation(
+                out=rstd[:, a : a + 1], in_=squares[:], func=ACT.Abs_reciprocal_sqrt, bias=EPS, scale=1.0 / K
+            )
+
+        def root(j):
+            if j != SCALAR_STATS:
+                neg_mean = stat_pool.tile([P, SIZES[j]], F32)
+                rstd = stat_pool.tile([P, SIZES[j]], F32)
+                factors[j] = (neg_mean, rstd)
+            neg_mean, rstd = factors[j]
+            n = vector_tiles(j)
+            nc.scalar.activation(
+                out=rstd[:, 0:n], in_=moments[j][:, 0:n, 1], func=ACT.Abs_reciprocal_sqrt, bias=EPS, scale=1.0
+            )
+            nc.scalar.activation(out=neg_mean[:, 0:n], in_=moments[j][:, 0:n, 0], func=ACT.Copy, scale=-1.0)
             for a in range(SIZES[j]):
                 if on_scalar(j, a):
                     shift = stat_pool.tile([P, 1], F32)
@@ -287,6 +321,10 @@ def tile_swidtblock_pa_t_kernel(
                     load(step + LOAD_AHEAD)
                 if 0 <= step - AHEAD < GROUPS:
                     turn(step - AHEAD)
+                if step + 2 == SCALAR_STATS:
+                    scalar_sum(SCALAR_STATS)
+                if step == SCALAR_STATS:
+                    scalar_square(SCALAR_STATS)
                 if 0 <= step - 1 < GROUPS:
                     root(step - 1)
                 if 0 <= step - AHEAD - 2:

from contextlib import ExitStack

import concourse.mybir as mybir
from concourse.masks import make_identity

F32 = mybir.dt.float32
BF16 = mybir.dt.bfloat16
I32 = mybir.dt.int32
U32 = mybir.dt.uint32
U8 = mybir.dt.uint8
FP8X4 = mybir.dt.float8_e4m3fn_x4
ALU = mybir.AluOpType
ACT = mybir.ActivationFunctionType

P = 128
PACK = 4
K_PASS = P * PACK
TOKENS = 4 * 1024
K = 1024
PASSES = K // K_PASS
PLANES = PASSES * PACK
WIDTH = 256
OUTS = 3
TILES = 2
SHORT = 2
SIZES = [1] * SHORT + [TILES] * (TOKENS // (TILES * P) - SHORT) + [1] * SHORT
GROUPS = len(SIZES)
STARTS = [P * sum(SIZES[:j]) for j in range(GROUPS)]
EPS = 1e-6
BN_MAX = 512
BN_CALLS = K // BN_MAX
BN_DIM = 6
LOAD_AHEAD = 5
SCALAR_STATS = 12
AHEAD = 3

FLOPS = 2 * TOKENS * K * OUTS * WIDTH


def tile_swidtblock_pa_t_kernel(
    tc, x, ln1_gain, ln1_bias, wq_words, wq_scales, bq, wk_words, wk_scales, bk, wv_words, wv_scales, bv,
    out_0, out_1, out_2,
):
    nc = tc.nc
    x_tokens = x.rearrange("b s k -> (b s) k")
    out_tokens = [o.rearrange("b s h d -> (b s) (h d)") for o in (out_0, out_1, out_2)]

    def group_rows(rows, j):
        return rows[STARTS[j] : STARTS[j] + SIZES[j] * P].rearrange("(q a) c -> q a c", a=SIZES[j])

    with ExitStack() as ctx:
        const = ctx.enter_context(tc.tile_pool(name="const", bufs=1))
        x_pool = ctx.enter_context(tc.tile_pool(name="x_pool", bufs=LOAD_AHEAD + 3))
        stat_pool = ctx.enter_context(tc.tile_pool(name="stat_pool", bufs=4))
        n_pool = ctx.enter_context(tc.tile_pool(name="n_pool", bufs=TILES * (AHEAD + 1)))
        h_pool = ctx.enter_context(tc.tile_pool(name="h_pool", bufs=3))
        scratch_pool = ctx.enter_context(tc.tile_pool(name="scratch_pool", bufs=2))
        o_pool = ctx.enter_context(tc.tile_pool(name="o_pool", bufs=4))
        t_psum = ctx.enter_context(tc.psum_pool(name="t_psum", bufs=1))
        acc_psum = ctx.enter_context(tc.psum_pool(name="acc_psum", bufs=2))

        loaded = {}

        def load(j):
            x_sb = x_pool.tile([P, SIZES[j], K], BF16)
            if j == 0:
                for c in range(BN_CALLS):
                    cols = slice(c * BN_MAX, (c + 1) * BN_MAX)
                    nc.sync.dma_start(out=x_sb[:, :, cols], in_=group_rows(x_tokens, j)[:, :, cols])
            else:
                nc.sync.dma_start(out=x_sb[:], in_=group_rows(x_tokens, j))
            loaded[j] = x_sb

        load(0)
        gain_bf = const.tile([P, PASSES, PACK], BF16)
        bias_bf = const.tile([P, PASSES, PACK], BF16)
        nc.sync.dma_start(out=gain_bf[:], in_=ln1_gain.rearrange("(g p t) -> p g t", g=PASSES, p=P))
        nc.sync.dma_start(out=bias_bf[:], in_=ln1_bias.rearrange("(g p t) -> p g t", g=PASSES, p=P))
        for j in range(1, LOAD_AHEAD):
            load(j)

        ident = const.tile([P, P], F32)
        make_identity(nc, ident[:])

        gain_pt = const.tile([P, PLANES], F32)
        bias_pt = const.tile([P, PLANES], F32)
        nc.vector.tensor_copy(out=gain_pt[:], in_=gain_bf[:].rearrange("p g t -> p (g t)"))
        nc.vector.tensor_copy(out=bias_pt[:], in_=bias_bf[:].rearrange("p g t -> p (g t)"))

        w_codes = const.tile([P, PASSES, OUTS * WIDTH], U32, align_bytes=64)
        w_scales = const.tile([P, PASSES, OUTS * WIDTH], U8, align_bytes=64)
        nc.vector.memset(w_scales[:].rearrange("p g n -> p (g n)").bitcast(I32), 0)
        for w, (words, scales) in enumerate(((wq_words, wq_scales), (wk_words, wk_scales), (wv_words, wv_scales))):
            cols = slice(w * WIDTH, (w + 1) * WIDTH)
            nc.sync.dma_start(
                out=w_codes[:, :, cols].bitcast(I32),
                in_=words.rearrange("g p n t -> p g (n t)").bitcast(I32),
            )
            for quad in range(4):
                nc.sync.dma_start(
                    out=w_scales[32 * quad : 32 * quad + 4, :, cols].bitcast(I32),
                    in_=scales[:, 4 * quad : 4 * quad + 4, :].rearrange("g r n -> r g n").bitcast(I32),
                )

        b_bf = const.tile([P, OUTS, WIDTH], BF16)
        for w, b in enumerate((bq, bk, bv)):
            nc.sync.dma_start(out=b_bf[:, w, :], in_=b.partition_broadcast(P))
        b_all = const.tile([P, OUTS, WIDTH], F32)
        nc.vector.tensor_copy(out=b_all[:], in_=b_bf[:])

        partial = {}
        moments = {}
        turned = {}
        quantised = {}
        products = {}
        normed = {}
        quantised_in = {}
        factors = {}
        shifts = {}
        last_bank = {}

        def late(j):
            return j == GROUPS - 1

        def vector_tiles(j):
            return SIZES[j] - 1 if j == SCALAR_STATS else SIZES[j]

        def on_scalar(j, a):
            return j == SHORT and a == TILES - 1

        def statistics(j):
            x_sb = loaded[j]
            stats = stat_pool.tile([P, SIZES[j], BN_CALLS, BN_DIM], F32)
            for a in range(vector_tiles(j)):
                for c in range(BN_CALLS):
                    nc.vector.bn_stats(out=stats[:, a, c, :], in_=x_sb[:, a, c * BN_MAX : (c + 1) * BN_MAX])
            partial[j] = stats

        def aggregate(j):
            mean_var = stat_pool.tile([P, SIZES[j], 2], F32)
            for a in range(vector_tiles(j)):
                nc.vector.bn_aggr(out=mean_var[:, a, :], in_=partial[j][:, a].rearrange("q c s -> q (c s)"))
            moments[j] = mean_var

        def scalar_sum(j):
            a = SIZES[j] - 1
            neg_mean = stat_pool.tile([P, SIZES[j]], F32, name="neg_mean")
            rstd = stat_pool.tile([P, SIZES[j]], F32, name="rstd")
            factors[j] = (neg_mean, rstd)
            total = stat_pool.tile([P, 1], F32)
            scratch = scratch_pool.tile([P, K], BF16)
            nc.scalar.activation(out=scratch[:], in_=loaded[j][:, a, :], func=ACT.Identity, accum_out=total[:])
            nc.scalar.activation(out=neg_mean[:, a : a + 1], in_=total[:], func=ACT.Copy, scale=-1.0 / K)

        def scalar_square(j):
            a = SIZES[j] - 1
            neg_mean, rstd = factors[j]
            squares = stat_pool.tile([P, 1], F32)
            scratch = scratch_pool.tile([P, K], BF16)
            nc.scalar.activation(
                out=scratch[:],
                in_=loaded[j][:, a, :],
                func=ACT.Square,
                bias=neg_mean[:, a : a + 1],
                accum_out=squares[:],
            )
            nc.scalar.activation(
                out=rstd[:, a : a + 1], in_=squares[:], func=ACT.Abs_reciprocal_sqrt, bias=EPS, scale=1.0 / K
            )

        def root(j):
            if j != SCALAR_STATS:
                neg_mean = stat_pool.tile([P, SIZES[j]], F32)
                rstd = stat_pool.tile([P, SIZES[j]], F32)
                factors[j] = (neg_mean, rstd)
            neg_mean, rstd = factors[j]
            n = vector_tiles(j)
            nc.scalar.activation(
                out=rstd[:, 0:n], in_=moments[j][:, 0:n, 1], func=ACT.Abs_reciprocal_sqrt, bias=EPS, scale=1.0
            )
            nc.scalar.activation(out=neg_mean[:, 0:n], in_=moments[j][:, 0:n, 0], func=ACT.Copy, scale=-1.0)
            for a in range(SIZES[j]):
                if on_scalar(j, a):
                    shift = stat_pool.tile([P, 1], F32)
                    nc.scalar.activation(
                        out=shift[:], in_=neg_mean[:, a : a + 1], func=ACT.Copy, scale=rstd[:, a : a + 1]
                    )
                    shifts[j] = shift

        def normalise(j):
            x_sb = loaded[j]
            neg_mean, rstd = factors[j]
            tiles = []
            for a in range(SIZES[j]):
                n_sb = n_pool.tile([P, PLANES, P], F32)
                if on_scalar(j, a):
                    nc.scalar.activation(
                        out=n_sb[:].rearrange("q (g t) p -> q g t p", g=PASSES),
                        in_=x_sb[:, a, :].rearrange("q (g p t) -> q g t p", g=PASSES, p=P),
                        func=ACT.Identity,
                        bias=shifts[j][:],
                        scale=rstd[:, a : a + 1],
                    )
                else:
                    nc.gpsimd.tensor_scalar(
                        out=n_sb[:].rearrange("q (g t) p -> q g t p", g=PASSES),
                        in0=x_sb[:, a, :].rearrange("q (g p t) -> q g t p", g=PASSES, p=P),
                        scalar1=neg_mean[:, a : a + 1],
                        scalar2=rstd[:, a : a + 1],
                        op0=ALU.add,
                        op1=ALU.mult,
                    )
                tiles.append(n_sb)
            normed[j] = tiles

        def turn(j):
            planes = h_pool.tile([P, PLANES, SIZES[j] * P], BF16)
            for bank in range(PLANES // 2):
                n_t = t_psum.tile([P, 2, SIZES[j] * P], F32, name="n_t%d" % bank)
                for half in range(2):
                    for a in range(SIZES[j]):
                        nc.tensor.transpose(
                            n_t[:, half, a * P : (a + 1) * P], normed[j][a][:, 2 * bank + half, :], ident[:]
                        )
                if late(j) and bank == PLANES // 2 - 1:
                    last_bank[j] = n_t
                else:
                    for half in range(2):
                        plane = 2 * bank + half
                        nc.scalar.activation(
                            out=planes[:, plane, :],
                            in_=n_t[:, half, :],
                            func=ACT.Identity,
                            bias=bias_pt[:, plane : plane + 1],
                            scale=gain_pt[:, plane : plane + 1],
                        )
            turned[j] = planes

        def turn_last(j):
            for half in range(2):
                plane = PLANES - 2 + half
                nc.vector.tensor_scalar(
                    out=turned[j][:, plane, :],
                    in0=last_bank[j][:, half, :],
                    scalar1=gain_pt[:, plane : plane + 1],
                    scalar2=bias_pt[:, plane : plane + 1],
                    op0=ALU.mult,
                    op1=ALU.add,
                )

        def regroup(j):
            planes = turned[j]
            tokens = SIZES[j] * P
            grouped = h_pool.tile([P, PASSES, tokens, PACK], BF16, align_bytes=64)
            nc.scalar.copy(
                out=grouped[:, 0].rearrange("p (c i) t -> p c t i", i=4),
                in_=planes[:, 0:PACK, :].rearrange("p t (c i) -> p c t i", i=4),
            )
            first = 0 if late(j) else tokens // 2
            if first > 0:
                nc.scalar.copy(
                    out=grouped[:, 1, 0:first, :].rearrange("p (c i) t -> p c t i", i=4),
                    in_=planes[:, PACK : 2 * PACK, 0:first].rearrange("p t (c i) -> p c t i", i=4),
                )
            nc.gpsimd.tensor_scalar(
                out=grouped[:, 1, first:tokens, :],
                in0=planes[:, PACK : 2 * PACK, first:tokens].rearrange("p t c -> p c t"),
                scalar1=1.0,
                scalar2=0.0,
                op0=ALU.mult,
                op1=ALU.add,
            )
            quantised_in[j] = grouped

        def quantise(j):
            h_codes = h_pool.tile([P, PASSES, SIZES[j] * P], U32, align_bytes=64)
            h_scales = h_pool.tile([P, PASSES, SIZES[j] * P], U8, align_bytes=64)
            nc.vector.quantize_mx(
                out=h_codes[:].rearrange("p g c -> p (g c)").bitcast(FP8X4),
                scales=h_scales[:].rearrange("p g c -> p (g c)"),
                in_=quantised_in[j][:].rearrange("p g c t -> p (g c t)"),
            )
            quantised[j] = (h_codes, h_scales)

        def multiply(j):
            h_codes, h_scales = quantised[j]
            acc_v = acc_psum.tile([P, SIZES[j], WIDTH], F32)
            accs_qk = []
            for a in range(SIZES[j]):
                toks = slice(a * P, (a + 1) * P)
                acc_qk = acc_psum.tile([P, 2, WIDTH], F32)
                for g in range(PASSES):
                    for acc, cols in ((acc_qk[:].rearrange("q w c -> q (w c)"), slice(0, 2 * WIDTH)),
                                      (acc_v[:, a, :], slice(2 * WIDTH, 3 * WIDTH))):
                        nc.tensor.matmul_mx(
                            out=acc,
                            lhsT=h_codes[:, g, toks].bitcast(FP8X4),
                            lhsT_scale=h_scales[:, g, toks],
                            rhs=w_codes[:, g, cols].bitcast(FP8X4),
                            rhs_scale=w_scales[:, g, cols],
                            start=(g == 0),
                            stop=(g == PASSES - 1),
                        )
                accs_qk.append(acc_qk)
            products[j] = (accs_qk, acc_v)

        def finish(j):
            accs_qk, acc_v = products[j]
            o_sb = o_pool.tile([P, OUTS, SIZES[j], WIDTH], F32)
            for a in range(SIZES[j]):
                nc.vector.tensor_tensor(out=o_sb[:, 0:2, a, :], in0=b_all[:, 0:2, :], in1=accs_qk[a][:], op=ALU.add)
            nc.vector.tensor_tensor(
                out=o_sb[:, 2], in0=b_all[:, 2:3, :].to_broadcast([P, SIZES[j], WIDTH]), in1=acc_v[:], op=ALU.add
            )
            for w in range(OUTS):
                nc.sync.dma_start(out=group_rows(out_tokens[w], j), in_=o_sb[:, w])

        with tc.manual_schedule():
            for step in range(GROUPS + AHEAD + 2):
                if step + LOAD_AHEAD < GROUPS:
                    load(step + LOAD_AHEAD)
                if 0 <= step - AHEAD < GROUPS:
                    turn(step - AHEAD)
                if step + 2 == SCALAR_STATS:
                    scalar_sum(SCALAR_STATS)
                if step == SCALAR_STATS:
                    scalar_square(SCALAR_STATS)
                if 0 <= step - 1 < GROUPS:
                    root(step - 1)
                if 0 <= step - AHEAD - 2:
                    multiply(step - AHEAD - 2)
                if 0 <= step - AHEAD - 1 < GROUPS:
                    quantise(step - AHEAD - 1)
                if step < GROUPS:
                    statistics(step)
                if 0 <= step - AHEAD < GROUPS and late(step - AHEAD):
                    turn_last(step - AHEAD)
                if 0 <= step - AHEAD < GROUPS:
                    regroup(step - AHEAD)
                if 0 <= step - 1 < GROUPS:
                    normalise(step - 1)
                if 0 <= step - AHEAD - 2:
                    finish(step - AHEAD - 2)
                if step < GROUPS:
                    aggregate(step)
